import numpy as np
import ml_dtypes


def mxq(x, axis, fmt="e4m3"):
    dtype, down = {"e4m3": (ml_dtypes.float8_e4m3fn, 7), "e5m2": (ml_dtypes.float8_e5m2, 14)}[fmt]
    v = np.moveaxis(np.asarray(x, np.float32).astype(ml_dtypes.bfloat16).astype(np.float64), axis, -1)
    blocks = v.reshape(v.shape[:-1] + (-1, 32))
    amax = np.abs(blocks).max(-1, keepdims=True)
    byte = np.maximum(np.where(amax > 0, np.frexp(amax)[1] - 1 + 127, 0) - down, 1)
    scale = np.exp2(byte - 127.0)
    codes = (blocks / scale).astype(np.float32).astype(dtype).astype(np.float64)
    return np.moveaxis((codes * scale).reshape(v.shape), -1, axis)


WIDE = False


def mx_kscale(k):
    if not WIDE:
        return np.ones(k)
    levels = np.array([10, -10, 5, -5, 0])
    a = np.random.permutation(np.resize(levels, k // 512 * 4)).reshape(k // 512, 4)
    idx = np.arange(k)
    return np.exp2(a[idx // 512, idx % 128 // 32])


BF16 = ml_dtypes.bfloat16


def bf(x):
    return np.asarray(x, np.float32).astype(BF16)


def f64(x):
    return np.asarray(x).astype(np.float64)


B, J, I, O = 1024, 8, 512, 128
IN_CH = J * I
OUT_CH = J * O
NEIGHBOUR_LIST = [[j for j in (i - 1, i, i + 1) if 0 <= j < J] for i in range(J)]


def build_mask():
    mask = np.zeros((OUT_CH, IN_CH))
    for i, neigh in enumerate(NEIGHBOUR_LIST):
        mask[i * O:(i + 1) * O, neigh[0] * I:(neigh[-1] + 1) * I] = 1.0
    return mask


def setup_inputs():
    s = mx_kscale(IN_CH)
    keep = np.random.random((OUT_CH, IN_CH)) < 0.75
    return {"x": bf(np.random.standard_normal((B, IN_CH)) * s),
            "weight": bf(np.random.standard_normal((OUT_CH, IN_CH)) / np.sqrt(0.75 * 3 * I) / s[None, :]),
            "mask": bf(build_mask() * keep),
            "bias": bf(np.random.standard_normal(OUT_CH) * 0.5)}


def reference(x, weight, mask, bias):
    x2 = f64(x).reshape(x.shape[0], -1)
    w = f64(weight) * f64(mask)
    xq = mxq(x2, 1, "e4m3")
    cols = []
    for i, neigh in enumerate(NEIGHBOUR_LIST):
        lo, hi = neigh[0] * I, (neigh[-1] + 1) * I
        cols.append(xq[:, lo:hi] @ mxq(w[i * O:(i + 1) * O, lo:hi], 1, "e4m3").T)
    return np.concatenate(cols, axis=1) + f64(bias)

@@ -1,0 +1,185 @@
+from contextlib import ExitStack
+
+import concourse.mybir as mybir
+from concourse.masks import make_identity
+
+F32 = mybir.dt.float32
+BF16 = mybir.dt.bfloat16
+U32 = mybir.dt.uint32
+U8 = mybir.dt.uint8
+FP8X4 = mybir.dt.float8_e4m3fn_x4
+ADD = mybir.AluOpType.add
+MULT = mybir.AluOpType.mult
+
+P = 128
+B, J, I, O = 1024, 8, 512, 128
+NT = B // P
+NBLK = 3 * J - 2
+FLOPS = 2 * B * O * I * NBLK
+BYTES = 2 * B * J * I + 2 * 2 * NBLK * O * I + 2 * J * O + 4 * B * J * O
+
+NF = 4
+LAG = 1
+
+
+def neighbours(i):
+    return list(range(max(i - 1, 0), min(i + 2, J)))
+
+
+def tile_skeletonlinear_kernel(tc, x, weight, mask, bias, out):
+    nc = tc.nc
+    with ExitStack() as ctx:
+        const = ctx.enter_context(tc.tile_pool(name="const", bufs=1))
+        keep = ctx.enter_context(tc.tile_pool(name="keep", bufs=1))
+        xraw = ctx.enter_context(tc.tile_pool(name="xraw", bufs=4))
+        grp = ctx.enter_context(tc.tile_pool(name="grp", bufs=3))
+        psum = ctx.enter_context(tc.psum_pool(name="psum", bufs=4))
+
+        x_view = x.rearrange("(p t) k -> p t k", t=NT)
+        out_view = out.rearrange("(p t) o -> p t o", t=NT)
+
+        ident = const.tile([P, P], F32, name="ident")
+        make_identity(nc, ident[:])
+        ones = const.tile([P, P], BF16, name="ones")
+        nc.vector.memset(ones[:], 1.0)
+        brow = const.tile([P, J * O], BF16, name="brow")
+        nc.vector.memset(brow[:], 0.0)
+        nc.scalar.dma_start(out=brow[0:1, :], in_=bias.rearrange("(a n) -> a n", a=1))
+        bias_bc = const.tile([P, J * O], F32, name="bias_bc")
+
+        xr = {}
+        wr = {}
+        mr = {}
+
+        def load_x(t):
+            xr[t] = xraw.tile([P, J * I], BF16, name="xr%d" % t, tag="xr")
+            nc.sync.dma_start(out=xr[t][:], in_=x_view[:, t, :])
+
+        def load_w(i):
+            ng = neighbours(i)
+            n = len(ng) * I
+            lo = ng[0] * I
+            wr[i] = keep.tile([P, n], BF16, name="wr%d" % i)
+            mr[i] = keep.tile([P, n], BF16, name="mr%d" % i)
+            nc.sync.dma_start(out=wr[i][:], in_=weight[i * O:(i + 1) * O, lo:lo + n])
+            nc.sync.dma_start(out=mr[i][:], in_=mask[i * O:(i + 1) * O, lo:lo + n])
+
+        for t in range(NF):
+            load_x(t)
+        for i in range(J):
+            load_w(i)
+
+        for h in range(2):
+            pb = psum.tile([P, 512], F32, name="pb", tag="acc")
+            nc.tensor.matmul(out=pb[:], lhsT=ones[:], rhs=brow[:, 512 * h:512 * (h + 1)], start=True, stop=True)
+            nc.vector.tensor_copy(out=bias_bc[:, 512 * h:512 * (h + 1)], in_=pb[:])
+
+        xc = {}
+        xs = {}
+        wc = {}
+        ws = {}
+
+        def transpose_group(src32, nblk, g32):
+            for b0 in range(0, nblk, 2):
+                nb = min(2, nblk - b0)
+                tp = psum.tile([P, 2, 2, P], F32, name="tp", tag="tp")
+                for gg in range(nb):
+                    for u in range(2):
+                        c0 = 256 * (b0 + gg) + 128 * u
+                        nc.tensor.transpose(out=tp[:, gg, u, :], in_=src32[:, c0:c0 + 128], identity=ident[:])
+                nc.scalar.copy(out=g32[:, b0:b0 + nb, :, :], in_=tp[:, 0:nb, :, :].rearrange("p g u r -> p g r u"))
+
+        def prep_x(t):
+            g = grp.tile([P, 4 * J * P], BF16, name="gx", tag="gx", align_bytes=64)
+            g32 = g[:].bitcast(F32).rearrange("p (g r u) -> p g r u", g=J, r=P, u=2)
+            transpose_group(xr[t][:].bitcast(F32), J, g32)
+            xc[t] = keep.tile([P, J * P], U32, name="xc%d" % t, align_bytes=64)
+            xs[t] = keep.tile([P, J * P], U8, name="xs%d" % t, align_bytes=64)
+            for h in range(2):
+                nc.vector.quantize_mx(
+                    out=xc[t][:, 512 * h:512 * (h + 1)].bitcast(FP8X4),
+                    scales=xs[t][:, 512 * h:512 * (h + 1)],
+                    in_=g[:, 2048 * h:2048 * (h + 1)],
+                )
+
+        def prep_w(i):
+            nblk = len(neighbours(i))
+            nc.vector.tensor_tensor(out=wr[i][:], in0=wr[i][:], in1=mr[i][:], op=MULT)
+            g = grp.tile([P, 4 * 3 * P], BF16, name="gw", tag="gw", align_bytes=64)
+            g32 = g[:].bitcast(F32).rearrange("p (g r u) -> p g r u", g=3, r=P, u=2)
+            transpose_group(wr[i][:].bitcast(F32), nblk, g32)
+            wc[i] = keep.tile([P, 3 * P], U32, name="wc%d" % i, align_bytes=64)
+            ws[i] = keep.tile([P, 3 * P], U8, name="ws%d" % i, align_bytes=64)
+            for b0 in range(0, nblk, 2):
+                nb = min(2, nblk - b0)
+                nc.vector.quantize_mx(
+                    out=wc[i][:, P * b0:P * (b0 + nb)].bitcast(FP8X4),
+                    scales=ws[i][:, P * b0:P * (b0 + nb)],
+                    in_=g[:, 4 * P * b0:4 * P * (b0 + nb)],
+                )
+
+        def cell(acc_ap, t, i):
+            ng = neighbours(i)
+            for gi, g in enumerate(ng):
+                nc.tensor.matmul_mx(
+                    out=acc_ap,
+                    lhsT=xc[t][:, P * g:P * (g + 1)].bitcast(FP8X4),
+                    lhsT_scale=xs[t][:, P * g:P * (g + 1)],
+                    rhs=wc[i][:, P * gi:P * (gi + 1)].bitcast(FP8X4),
+                    rhs_scale=ws[i][:, P * gi:P * (gi + 1)],
+                    start=(gi == 0),
+                    stop=(gi == len(ng) - 1),
+                )
+
+        osb_first = keep.tile([P, NF, J * O], F32, name="osb_first")
+
+        def cells_joint(i):
+            acc = psum.tile([P, 4, O], F32, name="acc", tag="acc")
+            for t in range(NF):
+                cell(acc[:, t, :], t, i)
+            nc.vector.tensor_tensor(
+                out=osb_first[:, :, O * i:O * (i + 1)],
+                in0=acc[:],
+                in1=bias_bc[:, O * i:O * (i + 1)].unsqueeze(1).to_broadcast([P, NF, O]),
+                op=ADD,
+            )
+
+        def cells_tile(t):
+            osb = keep.tile([P, J * O], F32, name="osb%d" % t)
+            for h in range(2):
+                acc = psum.tile([P, 4, O], F32, name="acc", tag="acc")
+                for c in range(4):
+                    cell(acc[:, c, :], t, 4 * h + c)
+                nc.vector.tensor_tensor(
+                    out=osb[:, 512 * h:512 * (h + 1)],
+                    in0=acc[:].rearrange("p c o -> p (c o)"),
+                    in1=bias_bc[:, 512 * h:512 * (h + 1)],
+                    op=ADD,
+                )
+            nc.sync.dma_start(out=out_view[:, t, :], in_=osb[:])
+
+        for t in range(NF):
+            prep_x(t)
+        for t in range(NF, NT):
+            load_x(t)
+
+        steps = [("w", i) for i in range(J)] + [("x", t) for t in range(NF, NT)]
+
+        def cells(step):
+            kind, idx = step
+            if kind == "w":
+                cells_joint(idx)
+                if idx == J - 1:
+                    nc.sync.dma_start(out=out_view[:, 0:NF, :], in_=osb_first[:])
+            else:
+                cells_tile(idx)
+
+        for n, (kind, idx) in enumerate(steps):
+            if kind == "w":
+                prep_w(idx)
+            else:
+                prep_x(idx)
+            if n >= LAG:
+                cells(steps[n - LAG])
+        for n in range(len(steps) - LAG, len(steps)):
+            cells(steps[n])

@@ -19,7 +19,6 @@ FLOPS = 2 * B * O * I * NBLK
 BYTES = 2 * B * J * I + 2 * 2 * NBLK * O * I + 2 * J * O + 4 * B * J * O
 
 NF = 4
-LAG = 1
 
 
 def neighbours(i):
@@ -33,7 +32,9 @@ def tile_skeletonlinear_kernel(tc, x, weight, mask, bias, out):
         keep = ctx.enter_context(tc.tile_pool(name="keep", bufs=1))
         xraw = ctx.enter_context(tc.tile_pool(name="xraw", bufs=4))
         grp = ctx.enter_context(tc.tile_pool(name="grp", bufs=3))
-        psum = ctx.enter_context(tc.psum_pool(name="psum", bufs=4))
+        psum_t = ctx.enter_context(tc.psum_pool(name="psum_t", bufs=4))
+        psum_a = ctx.enter_context(tc.psum_pool(name="psum_a", bufs=4))
+        ctx.enter_context(tc.manual_schedule())
 
         x_view = x.rearrange("(p t) k -> p t k", t=NT)
         out_view = out.rearrange("(p t) o -> p t o", t=NT)
@@ -44,12 +45,18 @@ def tile_skeletonlinear_kernel(tc, x, weight, mask, bias, out):
         nc.vector.memset(ones[:], 1.0)
         brow = const.tile([P, J * O], BF16, name="brow")
         nc.vector.memset(brow[:], 0.0)
-        nc.scalar.dma_start(out=brow[0:1, :], in_=bias.rearrange("(a n) -> a n", a=1))
+        nc.sync.dma_start(out=brow[0:1, :], in_=bias.rearrange("(a n) -> a n", a=1))
         bias_bc = const.tile([P, J * O], F32, name="bias_bc")
 
         xr = {}
         wr = {}
         mr = {}
+        gt = {}
+        xc = {}
+        xs = {}
+        wc = {}
+        ws = {}
+        accs = {}
 
         def load_x(t):
             xr[t] = xraw.tile([P, J * I], BF16, name="xr%d" % t, tag="xr")
@@ -64,59 +71,69 @@ def tile_skeletonlinear_kernel(tc, x, weight, mask, bias, out):
             nc.sync.dma_start(out=wr[i][:], in_=weight[i * O:(i + 1) * O, lo:lo + n])
             nc.sync.dma_start(out=mr[i][:], in_=mask[i * O:(i + 1) * O, lo:lo + n])
 
-        for t in range(NF):
-            load_x(t)
-        for i in range(J):
-            load_w(i)
+        def bias_spread():
+            for h in range(2):
+                pb = psum_a.tile([P, 512], F32, name="pb", tag="acc")
+                nc.tensor.matmul(out=pb[:], lhsT=ones[:], rhs=brow[:, 512 * h:512 * (h + 1)], start=True, stop=True)
+                nc.vector.tensor_copy(out=bias_bc[:, 512 * h:512 * (h + 1)], in_=pb[:])
 
-        for h in range(2):
-            pb = psum.tile([P, 512], F32, name="pb", tag="acc")
-            nc.tensor.matmul(out=pb[:], lhsT=ones[:], rhs=brow[:, 512 * h:512 * (h + 1)], start=True, stop=True)
-            nc.vector.tensor_copy(out=bias_bc[:, 512 * h:512 * (h + 1)], in_=pb[:])
-
-        xc = {}
-        xs = {}
-        wc = {}
-        ws = {}
-
-        def transpose_group(src32, nblk, g32):
+        def transpose_group(src32, nblk, g32, dve_banks):
             for b0 in range(0, nblk, 2):
                 nb = min(2, nblk - b0)
-                tp = psum.tile([P, 2, 2, P], F32, name="tp", tag="tp")
+                tp = psum_t.tile([P, 2, 2, P], F32, name="tp", tag="tp")
                 for gg in range(nb):
                     for u in range(2):
                         c0 = 256 * (b0 + gg) + 128 * u
                         nc.tensor.transpose(out=tp[:, gg, u, :], in_=src32[:, c0:c0 + 128], identity=ident[:])
-                nc.scalar.copy(out=g32[:, b0:b0 + nb, :, :], in_=tp[:, 0:nb, :, :].rearrange("p g u r -> p g r u"))
+                src = tp[:, 0:nb, :, :].rearrange("p g u r -> p g r u")
+                if b0 // 2 in dve_banks:
+                    nc.vector.tensor_copy(out=g32[:, b0:b0 + nb, :, :], in_=src)
+                else:
+                    nc.scalar.copy(out=g32[:, b0:b0 + nb, :, :], in_=src)
 
-        def prep_x(t):
-            g = grp.tile([P, 4 * J * P], BF16, name="gx", tag="gx", align_bytes=64)
-            g32 = g[:].bitcast(F32).rearrange("p (g r u) -> p g r u", g=J, r=P, u=2)
-            transpose_group(xr[t][:].bitcast(F32), J, g32)
-            xc[t] = keep.tile([P, J * P], U32, name="xc%d" % t, align_bytes=64)
-            xs[t] = keep.tile([P, J * P], U8, name="xs%d" % t, align_bytes=64)
-            for h in range(2):
-                nc.vector.quantize_mx(
-                    out=xc[t][:, 512 * h:512 * (h + 1)].bitcast(FP8X4),
-                    scales=xs[t][:, 512 * h:512 * (h + 1)],
-                    in_=g[:, 2048 * h:2048 * (h + 1)],
-                )
+        steps = [("x", t) for t in range(NF)] + [("w", i) for i in range(J)] + [("x", t) for t in range(NF, NT)]
+        N = len(steps)
 
-        def prep_w(i):
-            nblk = len(neighbours(i))
-            nc.vector.tensor_tensor(out=wr[i][:], in0=wr[i][:], in1=mr[i][:], op=MULT)
-            g = grp.tile([P, 4 * 3 * P], BF16, name="gw", tag="gw", align_bytes=64)
-            g32 = g[:].bitcast(F32).rearrange("p (g r u) -> p g r u", g=3, r=P, u=2)
-            transpose_group(wr[i][:].bitcast(F32), nblk, g32)
-            wc[i] = keep.tile([P, 3 * P], U32, name="wc%d" % i, align_bytes=64)
-            ws[i] = keep.tile([P, 3 * P], U8, name="ws%d" % i, align_bytes=64)
-            for b0 in range(0, nblk, 2):
-                nb = min(2, nblk - b0)
-                nc.vector.quantize_mx(
-                    out=wc[i][:, P * b0:P * (b0 + nb)].bitcast(FP8X4),
-                    scales=ws[i][:, P * b0:P * (b0 + nb)],
-                    in_=g[:, 4 * P * b0:4 * P * (b0 + nb)],
-                )
+        def stage_mask(step):
+            kind, i = step
+            if kind == "w":
+                nc.vector.tensor_tensor(out=wr[i][:], in0=wr[i][:], in1=mr[i][:], op=MULT)
+
+        def stage_transpose(step):
+            kind, n = step
+            if kind == "x":
+                g = grp.tile([P, 4 * J * P], BF16, name="gx", tag="gx", align_bytes=64)
+                g32 = g[:].bitcast(F32).rearrange("p (g r u) -> p g r u", g=J, r=P, u=2)
+                transpose_group(xr[n][:].bitcast(F32), J, g32, [])
+            else:
+                g = grp.tile([P, 4 * 3 * P], BF16, name="gw", tag="gw", align_bytes=64)
+                g32 = g[:].bitcast(F32).rearrange("p (g r u) -> p g r u", g=3, r=P, u=2)
+                transpose_group(wr[n][:].bitcast(F32), len(neighbours(n)), g32, [])
+            gt[step] = g
+
+        def stage_quantise(step):
+            kind, n = step
+            g = gt[step]
+            if kind == "x":
+                xc[n] = keep.tile([P, J * P], U32, name="xc%d" % n, align_bytes=64)
+                xs[n] = keep.tile([P, J * P], U8, name="xs%d" % n, align_bytes=64)
+                for h in range(2):
+                    nc.vector.quantize_mx(
+                        out=xc[n][:, 512 * h:512 * (h + 1)].bitcast(FP8X4),
+                        scales=xs[n][:, 512 * h:512 * (h + 1)],
+                        in_=g[:, 2048 * h:2048 * (h + 1)],
+                    )
+            else:
+                nblk = len(neighbours(n))
+                wc[n] = keep.tile([P, 3 * P], U32, name="wc%d" % n, align_bytes=64)
+                ws[n] = keep.tile([P, 3 * P], U8, name="ws%d" % n, align_bytes=64)
+                for b0 in range(0, nblk, 2):
+                    nb = min(2, nblk - b0)
+                    nc.vector.quantize_mx(
+                        out=wc[n][:, P * b0:P * (b0 + nb)].bitcast(FP8X4),
+                        scales=ws[n][:, P * b0:P * (b0 + nb)],
+                        in_=g[:, 4 * P * b0:4 * P * (b0 + nb)],
+                    )
 
         def cell(acc_ap, t, i):
             ng = neighbours(i)
@@ -131,55 +148,60 @@ def tile_skeletonlinear_kernel(tc, x, weight, mask, bias, out):
                     stop=(gi == len(ng) - 1),
                 )
 
+        def stage_multiply(step):
+            kind, n = step
+            if kind == "w":
+                acc = psum_a.tile([P, 4, O], F32, name="acc", tag="acc")
+                for t in range(NF):
+                    cell(acc[:, t, :], t, n)
+                accs[step] = [acc]
+            elif n >= NF:
+                accs[step] = []
+                for h in range(2):
+                    acc = psum_a.tile([P, 4, O], F32, name="acc", tag="acc")
+                    for c in range(4):
+                        cell(acc[:, c, :], n, 4 * h + c)
+                    accs[step] = accs[step] + [acc]
+
         osb_first = keep.tile([P, NF, J * O], F32, name="osb_first")
 
-        def cells_joint(i):
-            acc = psum.tile([P, 4, O], F32, name="acc", tag="acc")
-            for t in range(NF):
-                cell(acc[:, t, :], t, i)
-            nc.vector.tensor_tensor(
-                out=osb_first[:, :, O * i:O * (i + 1)],
-                in0=acc[:],
-                in1=bias_bc[:, O * i:O * (i + 1)].unsqueeze(1).to_broadcast([P, NF, O]),
-                op=ADD,
-            )
-
-        def cells_tile(t):
-            osb = keep.tile([P, J * O], F32, name="osb%d" % t)
-            for h in range(2):
-                acc = psum.tile([P, 4, O], F32, name="acc", tag="acc")
-                for c in range(4):
-                    cell(acc[:, c, :], t, 4 * h + c)
+        def stage_output(step):
+            kind, n = step
+            if kind == "w":
                 nc.vector.tensor_tensor(
-                    out=osb[:, 512 * h:512 * (h + 1)],
-                    in0=acc[:].rearrange("p c o -> p (c o)"),
-                    in1=bias_bc[:, 512 * h:512 * (h + 1)],
+                    out=osb_first[:, :, O * n:O * (n + 1)],
+                    in0=accs[step][0][:],
+                    in1=bias_bc[:, O * n:O * (n + 1)].unsqueeze(1).to_broadcast([P, NF, O]),
                     op=ADD,
                 )
-            nc.sync.dma_start(out=out_view[:, t, :], in_=osb[:])
+                if n == J - 1:
+                    nc.sync.dma_start(out=out_view[:, 0:NF, :], in_=osb_first[:])
+            elif n >= NF:
+                osb = keep.tile([P, J * O], F32, name="osb%d" % n)
+                for h in range(2):
+                    nc.vector.tensor_tensor(
+                        out=osb[:, 512 * h:512 * (h + 1)],
+                        in0=accs[step][h][:].rearrange("p c o -> p (c o)"),
+                        in1=bias_bc[:, 512 * h:512 * (h + 1)],
+                        op=ADD,
+                    )
+                nc.sync.dma_start(out=out_view[:, n, :], in_=osb[:])
 
         for t in range(NF):
-            prep_x(t)
-        for t in range(NF, NT):
             load_x(t)
+        for i in range(J):
+            load_w(i)
 
-        steps = [("w", i) for i in range(J)] + [("x", t) for t in range(NF, NT)]
-
-        def cells(step):
-            kind, idx = step
-            if kind == "w":
-                cells_joint(idx)
-                if idx == J - 1:
-                    nc.sync.dma_start(out=out_view[:, 0:NF, :], in_=osb_first[:])
-            else:
-                cells_tile(idx)
-
-        for n, (kind, idx) in enumerate(steps):
-            if kind == "w":
-                prep_w(idx)
-            else:
-                prep_x(idx)
-            if n >= LAG:
-                cells(steps[n - LAG])
-        for n in range(len(steps) - LAG, len(steps)):
-            cells(steps[n])
+        for n in range(N + 2):
+            if n < N:
+                stage_mask(steps[n])
+                stage_transpose(steps[n])
+                if n < NT - NF:
+                    load_x(NF + n)
+                if n == 0:
+                    bias_spread()
+            if 1 <= n <= N:
+                stage_quantise(steps[n - 1])
+                stage_multiply(steps[n - 1])
+            if n >= 2:
+                stage_output(steps[n - 2])

@@ -34,7 +34,6 @@ def tile_skeletonlinear_kernel(tc, x, weight, mask, bias, out):
         grp = ctx.enter_context(tc.tile_pool(name="grp", bufs=3))
         psum_t = ctx.enter_context(tc.psum_pool(name="psum_t", bufs=4))
         psum_a = ctx.enter_context(tc.psum_pool(name="psum_a", bufs=4))
-        ctx.enter_context(tc.manual_schedule())
 
         x_view = x.rearrange("(p t) k -> p t k", t=NT)
         out_view = out.rearrange("(p t) o -> p t o", t=NT)
@@ -45,7 +44,6 @@ def tile_skeletonlinear_kernel(tc, x, weight, mask, bias, out):
         nc.vector.memset(ones[:], 1.0)
         brow = const.tile([P, J * O], BF16, name="brow")
         nc.vector.memset(brow[:], 0.0)
-        nc.sync.dma_start(out=brow[0:1, :], in_=bias.rearrange("(a n) -> a n", a=1))
         bias_bc = const.tile([P, J * O], F32, name="bias_bc")
 
         xr = {}
@@ -185,10 +183,15 @@ def tile_skeletonlinear_kernel(tc, x, weight, mask, bias, out):
                         in1=bias_bc[:, 512 * h:512 * (h + 1)],
                         op=ADD,
                     )
-                nc.sync.dma_start(out=out_view[:, n, :], in_=osb[:])
+                    if n >= 6:
+                        nc.sync.dma_start(out=out_view[:, n, 512 * h:512 * (h + 1)], in_=osb[:, 512 * h:512 * (h + 1)])
+                if n < 6:
+                    nc.sync.dma_start(out=out_view[:, n, :], in_=osb[:])
 
         for t in range(NF):
             load_x(t)
+            if t == 0:
+                nc.sync.dma_start(out=brow[0:1, :], in_=bias.rearrange("(a n) -> a n", a=1))
         for i in range(J):
             load_w(i)
 
@@ -198,7 +201,7 @@ def tile_skeletonlinear_kernel(tc, x, weight, mask, bias, out):
                 stage_transpose(steps[n])
                 if n < NT - NF:
                     load_x(NF + n)
-                if n == 0:
+                if n == 1:
                     bias_spread()
             if 1 <= n <= N:
                 stage_quantise(steps[n - 1])

@@ -34,6 +34,7 @@ def tile_skeletonlinear_kernel(tc, x, weight, mask, bias, out):
         grp = ctx.enter_context(tc.tile_pool(name="grp", bufs=3))
         psum_t = ctx.enter_context(tc.psum_pool(name="psum_t", bufs=4))
         psum_a = ctx.enter_context(tc.psum_pool(name="psum_a", bufs=4))
+        ctx.enter_context(tc.manual_schedule())
 
         x_view = x.rearrange("(p t) k -> p t k", t=NT)
         out_view = out.rearrange("(p t) o -> p t o", t=NT)

@@ -196,7 +196,7 @@ def tile_skeletonlinear_kernel(tc, x, weight, mask, bias, out):
         for i in range(J):
             load_w(i)
 
-        for n in range(N + 2):
+        for n in range(N + 4):
             if n < N:
                 stage_mask(steps[n])
                 stage_transpose(steps[n])
@@ -204,8 +204,9 @@ def tile_skeletonlinear_kernel(tc, x, weight, mask, bias, out):
                     load_x(NF + n)
                 if n == 1:
                     bias_spread()
-            if 1 <= n <= N:
-                stage_quantise(steps[n - 1])
-                stage_multiply(steps[n - 1])
-            if n >= 2:
-                stage_output(steps[n - 2])
+            if 2 <= n < N + 2:
+                stage_quantise(steps[n - 2])
+            if n >= 4:
+                stage_output(steps[n - 4])
+            if 2 <= n < N + 2:
+                stage_multiply(steps[n - 2])

@@ -56,6 +56,7 @@ def tile_skeletonlinear_kernel(tc, x, weight, mask, bias, out):
         wc = {}
         ws = {}
         accs = {}
+        deferred = [None]
 
         def load_x(t):
             xr[t] = xraw.tile([P, J * I], BF16, name="xr%d" % t, tag="xr")
@@ -86,7 +87,7 @@ def tile_skeletonlinear_kernel(tc, x, weight, mask, bias, out):
                         nc.tensor.transpose(out=tp[:, gg, u, :], in_=src32[:, c0:c0 + 128], identity=ident[:])
                 src = tp[:, 0:nb, :, :].rearrange("p g u r -> p g r u")
                 if b0 // 2 in dve_banks:
-                    nc.vector.tensor_copy(out=g32[:, b0:b0 + nb, :, :], in_=src)
+                    deferred[0] = (g32[:, b0:b0 + nb, :, :], src)
                 else:
                     nc.scalar.copy(out=g32[:, b0:b0 + nb, :, :], in_=src)
 
@@ -103,7 +104,7 @@ def tile_skeletonlinear_kernel(tc, x, weight, mask, bias, out):
             if kind == "x":
                 g = grp.tile([P, 4 * J * P], BF16, name="gx", tag="gx", align_bytes=64)
                 g32 = g[:].bitcast(F32).rearrange("p (g r u) -> p g r u", g=J, r=P, u=2)
-                transpose_group(xr[n][:].bitcast(F32), J, g32, [])
+                transpose_group(xr[n][:].bitcast(F32), J, g32, [3])
             else:
                 g = grp.tile([P, 4 * 3 * P], BF16, name="gw", tag="gw", align_bytes=64)
                 g32 = g[:].bitcast(F32).rearrange("p (g r u) -> p g r u", g=3, r=P, u=2)
@@ -147,6 +148,9 @@ def tile_skeletonlinear_kernel(tc, x, weight, mask, bias, out):
                     stop=(gi == len(ng) - 1),
                 )
 
+        def group_width(t):
+            return 2 if t == NT - 1 else 4
+
         def stage_multiply(step):
             kind, n = step
             if kind == "w":
@@ -155,11 +159,12 @@ def tile_skeletonlinear_kernel(tc, x, weight, mask, bias, out):
                     cell(acc[:, t, :], t, n)
                 accs[step] = [acc]
             elif n >= NF:
+                width = group_width(n)
                 accs[step] = []
-                for h in range(2):
-                    acc = psum_a.tile([P, 4, O], F32, name="acc", tag="acc")
-                    for c in range(4):
-                        cell(acc[:, c, :], n, 4 * h + c)
+                for j0 in range(0, J, width):
+                    acc = psum_a.tile([P, width, O], F32, name="acc", tag="acc")
+                    for c in range(width):
+                        cell(acc[:, c, :], n, j0 + c)
                     accs[step] = accs[step] + [acc]
 
         osb_first = keep.tile([P, NF, J * O], F32, name="osb_first")
@@ -176,16 +181,18 @@ def tile_skeletonlinear_kernel(tc, x, weight, mask, bias, out):
                 if n == J - 1:
                     nc.sync.dma_start(out=out_view[:, 0:NF, :], in_=osb_first[:])
             elif n >= NF:
+                width = group_width(n)
                 osb = keep.tile([P, J * O], F32, name="osb%d" % n)
-                for h in range(2):
+                for k, j0 in enumerate(range(0, J, width)):
+                    cols = slice(O * j0, O * (j0 + width))
                     nc.vector.tensor_tensor(
-                        out=osb[:, 512 * h:512 * (h + 1)],
-                        in0=accs[step][h][:].rearrange("p c o -> p (c o)"),
-                        in1=bias_bc[:, 512 * h:512 * (h + 1)],
+                        out=osb[:, cols],
+                        in0=accs[step][k][:].rearrange("p c o -> p (c o)"),
+                        in1=bias_bc[:, cols],
                         op=ADD,
                     )
                     if n >= 6:
-                        nc.sync.dma_start(out=out_view[:, n, 512 * h:512 * (h + 1)], in_=osb[:, 512 * h:512 * (h + 1)])
+                        nc.sync.dma_start(out=out_view[:, n, cols], in_=osb[:, cols])
                 if n < 6:
                     nc.sync.dma_start(out=out_view[:, n, :], in_=osb[:])
 
@@ -196,7 +203,7 @@ def tile_skeletonlinear_kernel(tc, x, weight, mask, bias, out):
         for i in range(J):
             load_w(i)
 
-        for n in range(N + 4):
+        for n in range(N + 2):
             if n < N:
                 stage_mask(steps[n])
                 stage_transpose(steps[n])
@@ -204,9 +211,12 @@ def tile_skeletonlinear_kernel(tc, x, weight, mask, bias, out):
                     load_x(NF + n)
                 if n == 1:
                     bias_spread()
-            if 2 <= n < N + 2:
-                stage_quantise(steps[n - 2])
-            if n >= 4:
-                stage_output(steps[n - 4])
-            if 2 <= n < N + 2:
-                stage_multiply(steps[n - 2])
+            if 1 <= n <= N:
+                stage_quantise(steps[n - 1])
+            if n >= 2:
+                stage_output(steps[n - 2])
+            if 1 <= n <= N:
+                stage_multiply(steps[n - 1])
+            if deferred[0] is not None:
+                nc.vector.tensor_copy(out=deferred[0][0], in_=deferred[0][1])
+                deferred[0] = None

@@ -19,6 +19,7 @@ FLOPS = 2 * B * O * I * NBLK
 BYTES = 2 * B * J * I + 2 * 2 * NBLK * O * I + 2 * J * O + 4 * B * J * O
 
 NF = 4
+HALF = J * O // 2
 
 
 def neighbours(i):
@@ -56,28 +57,42 @@ def tile_skeletonlinear_kernel(tc, x, weight, mask, bias, out):
         wc = {}
         ws = {}
         accs = {}
-        deferred = [None]
 
-        def load_x(t):
-            xr[t] = xraw.tile([P, J * I], BF16, name="xr%d" % t, tag="xr")
-            nc.sync.dma_start(out=xr[t][:], in_=x_view[:, t, :])
+        steps = (
+            [("x", t) for t in range(NF)]
+            + [("w", i) for i in range(J - 1)]
+            + [("x", NF), ("w", J - 1)]
+            + [("x", t) for t in range(NF + 1, NT)]
+        )
+        N = len(steps)
+        cells_at = {}
+        for step in steps:
+            cells_at[step] = []
+            if step[0] == "w" or step[1] > NF:
+                cells_at[step] = [step]
+        cells_at[("w", J - 1)] = [("w", J - 1), ("x", NF)]
 
-        def load_w(i):
-            ng = neighbours(i)
-            n = len(ng) * I
-            lo = ng[0] * I
-            wr[i] = keep.tile([P, n], BF16, name="wr%d" % i)
-            mr[i] = keep.tile([P, n], BF16, name="mr%d" % i)
-            nc.sync.dma_start(out=wr[i][:], in_=weight[i * O:(i + 1) * O, lo:lo + n])
-            nc.sync.dma_start(out=mr[i][:], in_=mask[i * O:(i + 1) * O, lo:lo + n])
+        def load(step):
+            kind, n = step
+            if kind == "x":
+                xr[n] = xraw.tile([P, J * I], BF16, name="xr%d" % n, tag="xr")
+                nc.sync.dma_start(out=xr[n][:], in_=x_view[:, n, :])
+            else:
+                ng = neighbours(n)
+                width = len(ng) * I
+                lo = ng[0] * I
+                wr[n] = keep.tile([P, width], BF16, name="wr%d" % n)
+                mr[n] = keep.tile([P, width], BF16, name="mr%d" % n)
+                nc.sync.dma_start(out=wr[n][:], in_=weight[n * O:(n + 1) * O, lo:lo + width])
+                nc.sync.dma_start(out=mr[n][:], in_=mask[n * O:(n + 1) * O, lo:lo + width])
 
         def bias_spread():
             for h in range(2):
-                pb = psum_a.tile([P, 512], F32, name="pb", tag="acc")
-                nc.tensor.matmul(out=pb[:], lhsT=ones[:], rhs=brow[:, 512 * h:512 * (h + 1)], start=True, stop=True)
-                nc.vector.tensor_copy(out=bias_bc[:, 512 * h:512 * (h + 1)], in_=pb[:])
+                pb = psum_a.tile([P, HALF], F32, name="pb", tag="acc")
+                nc.tensor.matmul(out=pb[:], lhsT=ones[:], rhs=brow[:, HALF * h:HALF * (h + 1)], start=True, stop=True)
+                nc.vector.tensor_copy(out=bias_bc[:, HALF * h:HALF * (h + 1)], in_=pb[:])
 
-        def transpose_group(src32, nblk, g32, dve_banks):
+        def transpose_group(src32, nblk, g32):
             for b0 in range(0, nblk, 2):
                 nb = min(2, nblk - b0)
                 tp = psum_t.tile([P, 2, 2, P], F32, name="tp", tag="tp")
@@ -85,30 +100,19 @@ def tile_skeletonlinear_kernel(tc, x, weight, mask, bias, out):
                     for u in range(2):
                         c0 = 256 * (b0 + gg) + 128 * u
                         nc.tensor.transpose(out=tp[:, gg, u, :], in_=src32[:, c0:c0 + 128], identity=ident[:])
-                src = tp[:, 0:nb, :, :].rearrange("p g u r -> p g r u")
-                if b0 // 2 in dve_banks:
-                    deferred[0] = (g32[:, b0:b0 + nb, :, :], src)
-                else:
-                    nc.scalar.copy(out=g32[:, b0:b0 + nb, :, :], in_=src)
-
-        steps = [("x", t) for t in range(NF)] + [("w", i) for i in range(J)] + [("x", t) for t in range(NF, NT)]
-        N = len(steps)
-
-        def stage_mask(step):
-            kind, i = step
-            if kind == "w":
-                nc.vector.tensor_tensor(out=wr[i][:], in0=wr[i][:], in1=mr[i][:], op=MULT)
+                nc.scalar.copy(out=g32[:, b0:b0 + nb, :, :], in_=tp[:, 0:nb, :, :].rearrange("p g u r -> p g r u"))
 
         def stage_transpose(step):
             kind, n = step
             if kind == "x":
                 g = grp.tile([P, 4 * J * P], BF16, name="gx", tag="gx", align_bytes=64)
                 g32 = g[:].bitcast(F32).rearrange("p (g r u) -> p g r u", g=J, r=P, u=2)
-                transpose_group(xr[n][:].bitcast(F32), J, g32, [3])
+                transpose_group(xr[n][:].bitcast(F32), J, g32)
             else:
+                nc.vector.tensor_tensor(out=wr[n][:], in0=wr[n][:], in1=mr[n][:], op=MULT)
                 g = grp.tile([P, 4 * 3 * P], BF16, name="gw", tag="gw", align_bytes=64)
                 g32 = g[:].bitcast(F32).rearrange("p (g r u) -> p g r u", g=3, r=P, u=2)
-                transpose_group(wr[n][:].bitcast(F32), len(neighbours(n)), g32, [])
+                transpose_group(wr[n][:].bitcast(F32), len(neighbours(n)), g32)
             gt[step] = g
 
         def stage_quantise(step):
@@ -148,67 +152,65 @@ def tile_skeletonlinear_kernel(tc, x, weight, mask, bias, out):
                     stop=(gi == len(ng) - 1),
                 )
 
-        def group_width(t):
-            return 2 if t == NT - 1 else 4
-
         def stage_multiply(step):
-            kind, n = step
-            if kind == "w":
-                acc = psum_a.tile([P, 4, O], F32, name="acc", tag="acc")
-                for t in range(NF):
-                    cell(acc[:, t, :], t, n)
-                accs[step] = [acc]
-            elif n >= NF:
-                width = group_width(n)
-                accs[step] = []
-                for j0 in range(0, J, width):
-                    acc = psum_a.tile([P, width, O], F32, name="acc", tag="acc")
-                    for c in range(width):
-                        cell(acc[:, c, :], n, j0 + c)
-                    accs[step] = accs[step] + [acc]
+            for unit in cells_at[step]:
+                kind, n = unit
+                accs[unit] = []
+                if kind == "w":
+                    acc = psum_a.tile([P, 4, O], F32, name="acc", tag="acc")
+                    for t in range(NF):
+                        cell(acc[:, t, :], t, n)
+                    accs[unit] = [acc]
+                else:
+                    for h in range(2):
+                        acc = psum_a.tile([P, 4, O], F32, name="acc", tag="acc")
+                        for c in range(4):
+                            cell(acc[:, c, :], n, 4 * h + c)
+                        accs[unit] = accs[unit] + [acc]
 
         osb_first = keep.tile([P, NF, J * O], F32, name="osb_first")
 
         def stage_output(step):
-            kind, n = step
-            if kind == "w":
-                nc.vector.tensor_tensor(
-                    out=osb_first[:, :, O * n:O * (n + 1)],
-                    in0=accs[step][0][:],
-                    in1=bias_bc[:, O * n:O * (n + 1)].unsqueeze(1).to_broadcast([P, NF, O]),
-                    op=ADD,
-                )
-                if n == J - 1:
-                    nc.sync.dma_start(out=out_view[:, 0:NF, :], in_=osb_first[:])
-            elif n >= NF:
-                width = group_width(n)
-                osb = keep.tile([P, J * O], F32, name="osb%d" % n)
-                for k, j0 in enumerate(range(0, J, width)):
-                    cols = slice(O * j0, O * (j0 + width))
+            for unit in cells_at[step]:
+                kind, n = unit
+                if kind == "w":
                     nc.vector.tensor_tensor(
-                        out=osb[:, cols],
-                        in0=accs[step][k][:].rearrange("p c o -> p (c o)"),
-                        in1=bias_bc[:, cols],
+                        out=osb_first[:, :, O * n:O * (n + 1)],
+                        in0=accs[unit][0][:],
+                        in1=bias_bc[:, O * n:O * (n + 1)].unsqueeze(1).to_broadcast([P, NF, O]),
                         op=ADD,
                     )
-                    if n >= 6:
-                        nc.sync.dma_start(out=out_view[:, n, cols], in_=osb[:, cols])
-                if n < 6:
-                    nc.sync.dma_start(out=out_view[:, n, :], in_=osb[:])
+                    if n % 4 == 3:
+                        cols = slice(O * (n - 3), O * (n + 1))
+                        nc.sync.dma_start(out=out_view[:, 0:NF, cols], in_=osb_first[:, :, cols])
+                else:
+                    osb = keep.tile([P, J * O], F32, name="osb%d" % n)
+                    for h in range(2):
+                        cols = slice(HALF * h, HALF * (h + 1))
+                        nc.vector.tensor_tensor(
+                            out=osb[:, cols],
+                            in0=accs[unit][h][:].rearrange("p c o -> p (c o)"),
+                            in1=bias_bc[:, cols],
+                            op=ADD,
+                        )
+                        if n >= NT - 2:
+                            nc.sync.dma_start(out=out_view[:, n, cols], in_=osb[:, cols])
+                    if n < NT - 2:
+                        nc.sync.dma_start(out=out_view[:, n, :], in_=osb[:])
 
-        for t in range(NF):
-            load_x(t)
-            if t == 0:
+        early = NF + J - 1
+        for n in range(early):
+            load(steps[n])
+            if n == 0:
                 nc.sync.dma_start(out=brow[0:1, :], in_=bias.rearrange("(a n) -> a n", a=1))
-        for i in range(J):
-            load_w(i)
+        late = [[steps[early], steps[early + 1]]] + [[s] for s in steps[early + 2:]]
 
         for n in range(N + 2):
             if n < N:
-                stage_mask(steps[n])
                 stage_transpose(steps[n])
-                if n < NT - NF:
-                    load_x(NF + n)
+                if n < len(late):
+                    for s in late[n]:
+                        load(s)
                 if n == 1:
                     bias_spread()
             if 1 <= n <= N:
@@ -217,6 +219,3 @@ def tile_skeletonlinear_kernel(tc, x, weight, mask, bias, out):
                 stage_output(steps[n - 2])
             if 1 <= n <= N:
                 stage_multiply(steps[n - 1])
-            if deferred[0] is not None:
-                nc.vector.tensor_copy(out=deferred[0][0], in_=deferred[0][1])
-                deferred[0] = None

@@ -19,7 +19,6 @@ FLOPS = 2 * B * O * I * NBLK
 BYTES = 2 * B * J * I + 2 * 2 * NBLK * O * I + 2 * J * O + 4 * B * J * O
 
 NF = 4
-HALF = J * O // 2
 
 
 def neighbours(i):
@@ -37,8 +36,8 @@ def tile_skeletonlinear_kernel(tc, x, weight, mask, bias, out):
         psum_a = ctx.enter_context(tc.psum_pool(name="psum_a", bufs=4))
         ctx.enter_context(tc.manual_schedule())
 
-        x_view = x.rearrange("(p t) k -> p t k", t=NT)
-        out_view = out.rearrange("(p t) o -> p t o", t=NT)
+        x_view = x.rearrange("(t p) k -> p t k", p=P)
+        out_view = out.rearrange("(t p) o -> p t o", p=P)
 
         ident = const.tile([P, P], F32, name="ident")
         make_identity(nc, ident[:])
@@ -58,41 +57,26 @@ def tile_skeletonlinear_kernel(tc, x, weight, mask, bias, out):
         ws = {}
         accs = {}
 
-        steps = (
-            [("x", t) for t in range(NF)]
-            + [("w", i) for i in range(J - 1)]
-            + [("x", NF), ("w", J - 1)]
-            + [("x", t) for t in range(NF + 1, NT)]
-        )
-        N = len(steps)
-        cells_at = {}
-        for step in steps:
-            cells_at[step] = []
-            if step[0] == "w" or step[1] > NF:
-                cells_at[step] = [step]
-        cells_at[("w", J - 1)] = [("w", J - 1), ("x", NF)]
+        def load_x(t):
+            xr[t] = xraw.tile([P, J * I], BF16, name="xr%d" % t, tag="xr")
+            nc.sync.dma_start(out=xr[t][:], in_=x_view[:, t, :])
 
-        def load(step):
-            kind, n = step
-            if kind == "x":
-                xr[n] = xraw.tile([P, J * I], BF16, name="xr%d" % n, tag="xr")
-                nc.sync.dma_start(out=xr[n][:], in_=x_view[:, n, :])
-            else:
-                ng = neighbours(n)
-                width = len(ng) * I
-                lo = ng[0] * I
-                wr[n] = keep.tile([P, width], BF16, name="wr%d" % n)
-                mr[n] = keep.tile([P, width], BF16, name="mr%d" % n)
-                nc.sync.dma_start(out=wr[n][:], in_=weight[n * O:(n + 1) * O, lo:lo + width])
-                nc.sync.dma_start(out=mr[n][:], in_=mask[n * O:(n + 1) * O, lo:lo + width])
+        def load_w(i):
+            ng = neighbours(i)
+            n = len(ng) * I
+            lo = ng[0] * I
+            wr[i] = keep.tile([P, n], BF16, name="wr%d" % i)
+            mr[i] = keep.tile([P, n], BF16, name="mr%d" % i)
+            nc.sync.dma_start(out=wr[i][:], in_=weight[i * O:(i + 1) * O, lo:lo + n])
+            nc.sync.dma_start(out=mr[i][:], in_=mask[i * O:(i + 1) * O, lo:lo + n])
 
         def bias_spread():
             for h in range(2):
-                pb = psum_a.tile([P, HALF], F32, name="pb", tag="acc")
-                nc.tensor.matmul(out=pb[:], lhsT=ones[:], rhs=brow[:, HALF * h:HALF * (h + 1)], start=True, stop=True)
-                nc.vector.tensor_copy(out=bias_bc[:, HALF * h:HALF * (h + 1)], in_=pb[:])
+                pb = psum_a.tile([P, 512], F32, name="pb", tag="acc")
+                nc.tensor.matmul(out=pb[:], lhsT=ones[:], rhs=brow[:, 512 * h:512 * (h + 1)], start=True, stop=True)
+                nc.vector.tensor_copy(out=bias_bc[:, 512 * h:512 * (h + 1)], in_=pb[:])
 
-        def transpose_group(src32, nblk, g32):
+        def transpose_group(src32, nblk, g32, dve_banks):
             for b0 in range(0, nblk, 2):
                 nb = min(2, nblk - b0)
                 tp = psum_t.tile([P, 2, 2, P], F32, name="tp", tag="tp")
@@ -100,19 +84,30 @@ def tile_skeletonlinear_kernel(tc, x, weight, mask, bias, out):
                     for u in range(2):
                         c0 = 256 * (b0 + gg) + 128 * u
                         nc.tensor.transpose(out=tp[:, gg, u, :], in_=src32[:, c0:c0 + 128], identity=ident[:])
-                nc.scalar.copy(out=g32[:, b0:b0 + nb, :, :], in_=tp[:, 0:nb, :, :].rearrange("p g u r -> p g r u"))
+                src = tp[:, 0:nb, :, :].rearrange("p g u r -> p g r u")
+                if b0 // 2 in dve_banks:
+                    nc.vector.tensor_copy(out=g32[:, b0:b0 + nb, :, :], in_=src)
+                else:
+                    nc.scalar.copy(out=g32[:, b0:b0 + nb, :, :], in_=src)
+
+        steps = [("x", t) for t in range(NF)] + [("w", i) for i in range(J)] + [("x", t) for t in range(NF, NT)]
+        N = len(steps)
+
+        def stage_mask(step):
+            kind, i = step
+            if kind == "w":
+                nc.vector.tensor_tensor(out=wr[i][:], in0=wr[i][:], in1=mr[i][:], op=MULT)
 
         def stage_transpose(step):
             kind, n = step
             if kind == "x":
                 g = grp.tile([P, 4 * J * P], BF16, name="gx", tag="gx", align_bytes=64)
                 g32 = g[:].bitcast(F32).rearrange("p (g r u) -> p g r u", g=J, r=P, u=2)
-                transpose_group(xr[n][:].bitcast(F32), J, g32)
+                transpose_group(xr[n][:].bitcast(F32), J, g32, [])
             else:
-                nc.vector.tensor_tensor(out=wr[n][:], in0=wr[n][:], in1=mr[n][:], op=MULT)
                 g = grp.tile([P, 4 * 3 * P], BF16, name="gw", tag="gw", align_bytes=64)
                 g32 = g[:].bitcast(F32).rearrange("p (g r u) -> p g r u", g=3, r=P, u=2)
-                transpose_group(wr[n][:].bitcast(F32), len(neighbours(n)), g32)
+                transpose_group(wr[n][:].bitcast(F32), len(neighbours(n)), g32, [])
             gt[step] = g
 
         def stage_quantise(step):
@@ -153,69 +148,64 @@ def tile_skeletonlinear_kernel(tc, x, weight, mask, bias, out):
                 )
 
         def stage_multiply(step):
-            for unit in cells_at[step]:
-                kind, n = unit
-                accs[unit] = []
-                if kind == "w":
+            kind, n = step
+            if kind == "w":
+                acc = psum_a.tile([P, 4, O], F32, name="acc", tag="acc")
+                for t in range(NF):
+                    cell(acc[:, t, :], t, n)
+                accs[step] = [acc]
+            elif n >= NF:
+                accs[step] = []
+                for h in range(2):
                     acc = psum_a.tile([P, 4, O], F32, name="acc", tag="acc")
-                    for t in range(NF):
-                        cell(acc[:, t, :], t, n)
-                    accs[unit] = [acc]
-                else:
-                    for h in range(2):
-                        acc = psum_a.tile([P, 4, O], F32, name="acc", tag="acc")
-                        for c in range(4):
-                            cell(acc[:, c, :], n, 4 * h + c)
-                        accs[unit] = accs[unit] + [acc]
+                    for c in range(4):
+                        cell(acc[:, c, :], n, 4 * h + c)
+                    accs[step] = accs[step] + [acc]
 
         osb_first = keep.tile([P, NF, J * O], F32, name="osb_first")
 
         def stage_output(step):
-            for unit in cells_at[step]:
-                kind, n = unit
-                if kind == "w":
+            kind, n = step
+            if kind == "w":
+                nc.vector.tensor_tensor(
+                    out=osb_first[:, :, O * n:O * (n + 1)],
+                    in0=accs[step][0][:],
+                    in1=bias_bc[:, O * n:O * (n + 1)].unsqueeze(1).to_broadcast([P, NF, O]),
+                    op=ADD,
+                )
+                if n == J - 1:
+                    nc.sync.dma_start(out=out_view[:, 0:NF, :], in_=osb_first[:])
+            elif n >= NF:
+                osb = keep.tile([P, J * O], F32, name="osb%d" % n)
+                for h in range(2):
                     nc.vector.tensor_tensor(
-                        out=osb_first[:, :, O * n:O * (n + 1)],
-                        in0=accs[unit][0][:],
-                        in1=bias_bc[:, O * n:O * (n + 1)].unsqueeze(1).to_broadcast([P, NF, O]),
+                        out=osb[:, 512 * h:512 * (h + 1)],
+                        in0=accs[step][h][:].rearrange("p c o -> p (c o)"),
+                        in1=bias_bc[:, 512 * h:512 * (h + 1)],
                         op=ADD,
                     )
-                    if n % 4 == 3:
-                        cols = slice(O * (n - 3), O * (n + 1))
-                        nc.sync.dma_start(out=out_view[:, 0:NF, cols], in_=osb_first[:, :, cols])
-                else:
-                    osb = keep.tile([P, J * O], F32, name="osb%d" % n)
-                    for h in range(2):
-                        cols = slice(HALF * h, HALF * (h + 1))
-                        nc.vector.tensor_tensor(
-                            out=osb[:, cols],
-                            in0=accs[unit][h][:].rearrange("p c o -> p (c o)"),
-                            in1=bias_bc[:, cols],
-                            op=ADD,
-                        )
-                        if n >= NT - 2:
-                            nc.sync.dma_start(out=out_view[:, n, cols], in_=osb[:, cols])
-                    if n < NT - 2:
-                        nc.sync.dma_start(out=out_view[:, n, :], in_=osb[:])
+                    if n >= 6:
+                        nc.sync.dma_start(out=out_view[:, n, 512 * h:512 * (h + 1)], in_=osb[:, 512 * h:512 * (h + 1)])
+                if n < 6:
+                    nc.sync.dma_start(out=out_view[:, n, :], in_=osb[:])
 
-        early = NF + J - 1
-        for n in range(early):
-            load(steps[n])
-            if n == 0:
+        for t in range(NF):
+            load_x(t)
+            if t == 0:
                 nc.sync.dma_start(out=brow[0:1, :], in_=bias.rearrange("(a n) -> a n", a=1))
-        late = [[steps[early], steps[early + 1]]] + [[s] for s in steps[early + 2:]]
+        for i in range(J):
+            load_w(i)
 
         for n in range(N + 2):
             if n < N:
+                stage_mask(steps[n])
                 stage_transpose(steps[n])
-                if n < len(late):
-                    for s in late[n]:
-                        load(s)
+                if n < NT - NF:
+                    load_x(NF + n)
                 if n == 1:
                     bias_spread()
             if 1 <= n <= N:
                 stage_quantise(steps[n - 1])
+                stage_multiply(steps[n - 1])
             if n >= 2:
                 stage_output(steps[n - 2])
-            if 1 <= n <= N:
-                stage_multiply(steps[n - 1])

from contextlib import ExitStack

import concourse.mybir as mybir
from concourse.masks import make_identity

F32 = mybir.dt.float32
BF16 = mybir.dt.bfloat16
U32 = mybir.dt.uint32
U8 = mybir.dt.uint8
FP8X4 = mybir.dt.float8_e4m3fn_x4
ADD = mybir.AluOpType.add
MULT = mybir.AluOpType.mult

P = 128
B, J, I, O = 1024, 8, 512, 128
NT = B // P
NBLK = 3 * J - 2
FLOPS = 2 * B * O * I * NBLK
BYTES = 2 * B * J * I + 2 * 2 * NBLK * O * I + 2 * J * O + 4 * B * J * O

NF = 4


def neighbours(i):
    return list(range(max(i - 1, 0), min(i + 2, J)))


def tile_skeletonlinear_kernel(tc, x, weight, mask, bias, out):
    nc = tc.nc
    with ExitStack() as ctx:
        const = ctx.enter_context(tc.tile_pool(name="const", bufs=1))
        keep = ctx.enter_context(tc.tile_pool(name="keep", bufs=1))
        xraw = ctx.enter_context(tc.tile_pool(name="xraw", bufs=4))
        grp = ctx.enter_context(tc.tile_pool(name="grp", bufs=3))
        psum_t = ctx.enter_context(tc.psum_pool(name="psum_t", bufs=4))
        psum_a = ctx.enter_context(tc.psum_pool(name="psum_a", bufs=4))
        ctx.enter_context(tc.manual_schedule())

        x_view = x.rearrange("(t p) k -> p t k", p=P)
        out_view = out.rearrange("(t p) o -> p t o", p=P)

        ident = const.tile([P, P], F32, name="ident")
        make_identity(nc, ident[:])
        ones = const.tile([P, P], BF16, name="ones")
        nc.vector.memset(ones[:], 1.0)
        brow = const.tile([P, J * O], BF16, name="brow")
        nc.vector.memset(brow[:], 0.0)
        bias_bc = const.tile([P, J * O], F32, name="bias_bc")

        xr = {}
        wr = {}
        mr = {}
        gt = {}
        xc = {}
        xs = {}
        wc = {}
        ws = {}
        accs = {}

        def load_x(t):
            xr[t] = xraw.tile([P, J * I], BF16, name="xr%d" % t, tag="xr")
            nc.sync.dma_start(out=xr[t][:], in_=x_view[:, t, :])

        def load_w(i):
            ng = neighbours(i)
            n = len(ng) * I
            lo = ng[0] * I
            wr[i] = keep.tile([P, n], BF16, name="wr%d" % i)
            mr[i] = keep.tile([P, n], BF16, name="mr%d" % i)
            nc.sync.dma_start(out=wr[i][:], in_=weight[i * O:(i + 1) * O, lo:lo + n])
            nc.sync.dma_start(out=mr[i][:], in_=mask[i * O:(i + 1) * O, lo:lo + n])

        def bias_spread():
            for h in range(2):
                pb = psum_a.tile([P, 512], F32, name="pb", tag="acc")
                nc.tensor.matmul(out=pb[:], lhsT=ones[:], rhs=brow[:, 512 * h:512 * (h + 1)], start=True, stop=True)
                nc.vector.tensor_copy(out=bias_bc[:, 512 * h:512 * (h + 1)], in_=pb[:])

        def transpose_group(src32, nblk, g32, dve_banks):
            for b0 in range(0, nblk, 2):
                nb = min(2, nblk - b0)
                tp = psum_t.tile([P, 2, 2, P], F32, name="tp", tag="tp")
                for gg in range(nb):
                    for u in range(2):
                        c0 = 256 * (b0 + gg) + 128 * u
                        nc.tensor.transpose(out=tp[:, gg, u, :], in_=src32[:, c0:c0 + 128], identity=ident[:])
                src = tp[:, 0:nb, :, :].rearrange("p g u r -> p g r u")
                if b0 // 2 in dve_banks:
                    nc.vector.tensor_copy(out=g32[:, b0:b0 + nb, :, :], in_=src)
                else:
                    nc.scalar.copy(out=g32[:, b0:b0 + nb, :, :], in_=src)

        steps = [("x", t) for t in range(NF)] + [("w", i) for i in range(J)] + [("x", t) for t in range(NF, NT)]
        N = len(steps)

        def stage_mask(step):
            kind, i = step
            if kind == "w":
                nc.vector.tensor_tensor(out=wr[i][:], in0=wr[i][:], in1=mr[i][:], op=MULT)

        def stage_transpose(step):
            kind, n = step
            if kind == "x":
                g = grp.tile([P, 4 * J * P], BF16, name="gx", tag="gx", align_bytes=64)
                g32 = g[:].bitcast(F32).rearrange("p (g r u) -> p g r u", g=J, r=P, u=2)
                transpose_group(xr[n][:].bitcast(F32), J, g32, [])
            else:
                g = grp.tile([P, 4 * 3 * P], BF16, name="gw", tag="gw", align_bytes=64)
                g32 = g[:].bitcast(F32).rearrange("p (g r u) -> p g r u", g=3, r=P, u=2)
                transpose_group(wr[n][:].bitcast(F32), len(neighbours(n)), g32, [])
            gt[step] = g

        def stage_quantise(step):
            kind, n = step
            g = gt[step]
            if kind == "x":
                xc[n] = keep.tile([P, J * P], U32, name="xc%d" % n, align_bytes=64)
                xs[n] = keep.tile([P, J * P], U8, name="xs%d" % n, align_bytes=64)
                for h in range(2):
                    nc.vector.quantize_mx(
                        out=xc[n][:, 512 * h:512 * (h + 1)].bitcast(FP8X4),
                        scales=xs[n][:, 512 * h:512 * (h + 1)],
                        in_=g[:, 2048 * h:2048 * (h + 1)],
                    )
            else:
                nblk = len(neighbours(n))
                wc[n] = keep.tile([P, 3 * P], U32, name="wc%d" % n, align_bytes=64)
                ws[n] = keep.tile([P, 3 * P], U8, name="ws%d" % n, align_bytes=64)
                for b0 in range(0, nblk, 2):
                    nb = min(2, nblk - b0)
                    nc.vector.quantize_mx(
                        out=wc[n][:, P * b0:P * (b0 + nb)].bitcast(FP8X4),
                        scales=ws[n][:, P * b0:P * (b0 + nb)],
                        in_=g[:, 4 * P * b0:4 * P * (b0 + nb)],
                    )

        def cell(acc_ap, t, i):
            ng = neighbours(i)
            for gi, g in enumerate(ng):
                nc.tensor.matmul_mx(
                    out=acc_ap,
                    lhsT=xc[t][:, P * g:P * (g + 1)].bitcast(FP8X4),
                    lhsT_scale=xs[t][:, P * g:P * (g + 1)],
                    rhs=wc[i][:, P * gi:P * (gi + 1)].bitcast(FP8X4),
                    rhs_scale=ws[i][:, P * gi:P * (gi + 1)],
                    start=(gi == 0),
                    stop=(gi == len(ng) - 1),
                )

        def stage_multiply(step):
            kind, n = step
            if kind == "w":
                acc = psum_a.tile([P, 4, O], F32, name="acc", tag="acc")
                for t in range(NF):
                    cell(acc[:, t, :], t, n)
                accs[step] = [acc]
            elif n >= NF:
                accs[step] = []
                for h in range(2):
                    acc = psum_a.tile([P, 4, O], F32, name="acc", tag="acc")
                    for c in range(4):
                        cell(acc[:, c, :], n, 4 * h + c)
                    accs[step] = accs[step] + [acc]

        osb_first = keep.tile([P, NF, J * O], F32, name="osb_first")

        def stage_output(step):
            kind, n = step
            if kind == "w":
                nc.vector.tensor_tensor(
                    out=osb_first[:, :, O * n:O * (n + 1)],
                    in0=accs[step][0][:],
                    in1=bias_bc[:, O * n:O * (n + 1)].unsqueeze(1).to_broadcast([P, NF, O]),
                    op=ADD,
                )
                if n == J - 1:
                    nc.sync.dma_start(out=out_view[:, 0:NF, :], in_=osb_first[:])
            elif n >= NF:
                osb = keep.tile([P, J * O], F32, name="osb%d" % n)
                for h in range(2):
                    nc.vector.tensor_tensor(
                        out=osb[:, 512 * h:512 * (h + 1)],
                        in0=accs[step][h][:].rearrange("p c o -> p (c o)"),
                        in1=bias_bc[:, 512 * h:512 * (h + 1)],
                        op=ADD,
                    )
                    if n >= 6:
                        nc.sync.dma_start(out=out_view[:, n, 512 * h:512 * (h + 1)], in_=osb[:, 512 * h:512 * (h + 1)])
                if n < 6:
                    nc.sync.dma_start(out=out_view[:, n, :], in_=osb[:])

        for t in range(NF):
            load_x(t)
            if t == 0:
                nc.sync.dma_start(out=brow[0:1, :], in_=bias.rearrange("(a n) -> a n", a=1))
        for i in range(J):
            load_w(i)

        for n in range(N + 2):
            if n < N:
                stage_mask(steps[n])
                stage_transpose(steps[n])
                if n < NT - NF:
                    load_x(NF + n)
                if n == 1:
                    bias_spread()
            if 1 <= n <= N:
                stage_quantise(steps[n - 1])
                stage_multiply(steps[n - 1])
            if n >= 2:
                stage_output(steps[n - 2])
